import numpy as np
import ml_dtypes


def mxq(x, axis, fmt="e4m3"):
    dtype, down = {"e4m3": (ml_dtypes.float8_e4m3fn, 7), "e5m2": (ml_dtypes.float8_e5m2, 14)}[fmt]
    v = np.moveaxis(np.asarray(x, np.float32).astype(ml_dtypes.bfloat16).astype(np.float64), axis, -1)
    blocks = v.reshape(v.shape[:-1] + (-1, 32))
    amax = np.abs(blocks).max(-1, keepdims=True)
    byte = np.maximum(np.where(amax > 0, np.frexp(amax)[1] - 1 + 127, 0) - down, 1)
    scale = np.exp2(byte - 127.0)
    codes = (blocks / scale).astype(np.float32).astype(dtype).astype(np.float64)
    return np.moveaxis((codes * scale).reshape(v.shape), -1, axis)


WIDE = False


def mx_kscale(k):
    if not WIDE:
        return np.ones(k)
    levels = np.array([10, -10, 5, -5, 0])
    if k % 512:
        return np.exp2(np.random.permutation(np.resize(levels, k // 32))).repeat(32)
    a = np.empty((k // 512, 16))
    for p in range(k // 512):
        a[p, :8] = np.random.permutation(np.resize(levels, 8))
        for g in range(8):
            far = levels[np.abs(levels - a[p, g]) >= 10]
            a[p, g + 8] = far[np.random.randint(len(far))]
    return np.exp2(a.ravel()).repeat(32)


BF16 = ml_dtypes.bfloat16


def bf(x):
    return np.asarray(x, np.float32).astype(BF16)


def f64(x):
    return np.asarray(x).astype(np.float64)


B, L, D, H = 1, 1024, 512, 8
LN_EPS = 1e-5


def setup_inputs():
    s = mx_kscale(H * D)
    return {"heads": bf(np.random.standard_normal((H, L, D)) * 0.25 * s.reshape(H, D)[:, None, :]),
            "q": bf(np.random.standard_normal((B, L, D))),
            "proj_w": bf(np.random.standard_normal((D, H * D)) * 4.0 / np.sqrt(H * D) / s[None, :]),
            "proj_b": bf(np.random.standard_normal(D) * 0.1),
            "ln_gamma": bf(1.0 + np.random.standard_normal(D) * 0.1),
            "ln_beta": bf(np.random.standard_normal(D) * 0.1)}


def reference(heads, q, proj_w, proj_b, ln_gamma, ln_beta):
    hc = f64(heads).transpose(1, 0, 2).reshape(B, L, H * D)
    o = (mxq(hc, 2, "e4m3") @ mxq(f64(proj_w), 1, "e4m3").T) + f64(proj_b)
    x = o + f64(q)
    mu = x.mean(-1, keepdims=True)
    var = ((x - mu) ** 2).mean(-1, keepdims=True)
    return (x - mu) / np.sqrt(var + LN_EPS) * f64(ln_gamma) + f64(ln_beta)

@@ -1,0 +1,247 @@
+from contextlib import ExitStack
+
+import concourse.mybir as mybir
+from concourse.masks import make_identity
+
+FLOPS = 2 * 1024 * 4096 * 512
+
+F32 = mybir.dt.float32
+BF16 = mybir.dt.bfloat16
+U32 = mybir.dt.uint32
+U8 = mybir.dt.uint8
+FP8X4 = mybir.dt.float8_e4m3fn_x4
+ADD = mybir.AluOpType.add
+MULT = mybir.AluOpType.mult
+SQUARE = mybir.ActivationFunctionType.Square
+INV_SQRT = mybir.ActivationFunctionType.Abs_reciprocal_sqrt
+
+P = 128
+HEADS = 8
+ROWS = 1024
+FEAT = 512
+LN_EPS = 1e-5
+
+STRIPS = 8
+BANK_STRIPS = 2
+PIECES = STRIPS // BANK_STRIPS
+QUANT_STRIPS = 4
+TILES = 2
+GROUPS = ROWS // (TILES * P)
+X_HEADS = STRIPS // TILES
+W_HEADS = STRIPS * P // FEAT
+
+
+def tile_multiheadattention_pb_kernel(tc, heads, q, proj_w, proj_b, ln_gamma, ln_beta, out):
+    nc = tc.nc
+    q_rows = q.flatten_outer_dims()
+    out_rows = out.flatten_outer_dims()
+
+    with ExitStack() as ctx:
+        ctx.enter_context(tc.manual_schedule())
+        const = ctx.enter_context(tc.tile_pool(name="const", bufs=1))
+        raw = ctx.enter_context(tc.tile_pool(name="raw", bufs=1))
+        stage = ctx.enter_context(tc.tile_pool(name="stage", bufs=3))
+        operands = ctx.enter_context(tc.tile_pool(name="operands", bufs=3))
+        rows_pool = ctx.enter_context(tc.tile_pool(name="rows", bufs=4))
+        stats = ctx.enter_context(tc.tile_pool(name="stats", bufs=4))
+        banks = ctx.enter_context(tc.psum_pool(name="banks", bufs=4))
+        sums = ctx.enter_context(tc.psum_pool(name="sums", bufs=4))
+
+        ident = const.tile([P, P], F32)
+        make_identity(nc, ident[:])
+        ones = const.tile([P, P], BF16)
+        nc.vector.memset(ones[:], 1.0)
+        eps = const.tile([P, 1], F32)
+        nc.vector.memset(eps[:], LN_EPS)
+        vector_rows = const.tile([P, 3, FEAT], BF16)
+        nc.vector.memset(vector_rows[:], 0.0)
+        for j, vector in enumerate((proj_b, ln_gamma, ln_beta)):
+            nc.scalar.dma_start(out=vector_rows[0:1, j, :], in_=vector.rearrange("(o n) -> o n", o=1))
+        warm = const.tile([P, 1], F32)
+        nc.scalar.activation(out=warm[:], in_=eps[:], func=INV_SQRT)
+
+        w_raw = []
+        x_raw = {}
+        q_raw = []
+
+        def load_w(c):
+            pieces = []
+            for b in range(PIECES):
+                piece = raw.tile([P, BANK_STRIPS * FEAT], BF16, name="w_raw%d_%d" % (c, b))
+                nc.sync.dma_start(
+                    out=piece[:], in_=proj_w[b * P : (b + 1) * P, c * W_HEADS * FEAT : (c + 1) * W_HEADS * FEAT]
+                )
+                pieces.append(piece)
+            w_raw.append(pieces)
+
+        def load_x(g, c):
+            pieces = []
+            for b in range(PIECES):
+                piece = raw.tile([P, BANK_STRIPS * FEAT], BF16, name="x_raw%d_%d_%d" % (g, c, b))
+                nc.sync.dma_start(
+                    out=piece[:],
+                    in_=heads[c * X_HEADS + b, g * TILES * P : (g + 1) * TILES * P, :].rearrange(
+                        "(p t) d -> p (t d)", t=TILES
+                    ),
+                )
+                pieces.append(piece)
+            x_raw[(g, c)] = pieces
+
+        def load_q(g):
+            q_group = raw.tile([P, TILES * FEAT], BF16, name="q_raw%d" % g)
+            nc.sync.dma_start(
+                out=q_group[:],
+                in_=q_rows[g * TILES * P : (g + 1) * TILES * P, :].rearrange("(p t) n -> p (t n)", t=TILES),
+            )
+            q_raw.append(q_group)
+
+        load_w(0)
+        load_x(0, 0)
+        load_w(1)
+        load_w(2)
+        load_x(0, 1)
+        load_w(3)
+        load_q(0)
+        for g in range(1, GROUPS):
+            load_q(g)
+            load_x(g, 0)
+            load_x(g, 1)
+
+        bias_all = const.tile([P, FEAT], F32)
+        gamma_all = const.tile([P, FEAT], F32)
+        beta_all = const.tile([P, FEAT], F32)
+
+        def spread_vectors():
+            for j, spread in enumerate((bias_all, gamma_all, beta_all)):
+                bank = banks.tile([P, FEAT], F32, tag="bank")
+                nc.tensor.matmul(out=bank[:], lhsT=ones[:], rhs=vector_rows[:, j, :], start=True, stop=True)
+                nc.vector.tensor_copy(out=spread[:], in_=bank[:])
+
+        w_codes = const.tile([P, HEADS * FEAT], U32, align_bytes=64)
+        w_scales = const.tile([P, HEADS * FEAT], U8, align_bytes=64)
+        x_operands = {}
+        heads_done = [0] * GROUPS
+        acc = {}
+        residual = {}
+        centred = {}
+
+        def prepare(pieces, order, codes, scales):
+            grouped = stage.tile([P, STRIPS * FEAT], BF16, align_bytes=64)
+            places = grouped[:].bitcast(F32).rearrange(order, a=BANK_STRIPS, b=PIECES, u=2)
+            for b in range(PIECES):
+                words = pieces[b][:].bitcast(F32)
+                bank = banks.tile([P, FEAT], F32, tag="bank")
+                for j in range(BANK_STRIPS * 2):
+                    a, u = divmod(j, 2)
+                    nc.tensor.transpose(
+                        bank[:, j * P : (j + 1) * P], words[:, a * 2 * P + u : (a + 1) * 2 * P : 2], ident[:]
+                    )
+                nc.scalar.copy(out=places[:, b, :, :, :], in_=bank[:].rearrange("p (a u r) -> p a r u", a=BANK_STRIPS, u=2))
+            for s in range(0, STRIPS, QUANT_STRIPS):
+                nc.vector.quantize_mx(
+                    out=codes[:, s * P : (s + QUANT_STRIPS) * P].bitcast(FP8X4),
+                    scales=scales[:, s * P : (s + QUANT_STRIPS) * P],
+                    in_=grouped[:, s * FEAT : (s + QUANT_STRIPS) * FEAT],
+                )
+
+        def prepare_w(c):
+            columns = slice(c * STRIPS * P, (c + 1) * STRIPS * P)
+            prepare(w_raw[c], "p (a b r u) -> p b a r u", w_codes[:, columns], w_scales[:, columns])
+
+        def prepare_x(g, c):
+            x_codes = operands.tile([P, STRIPS * P], U32, align_bytes=64)
+            x_scales = operands.tile([P, STRIPS * P], U8, align_bytes=64)
+            prepare(x_raw[(g, c)], "p (b a r u) -> p b a r u", x_codes[:], x_scales[:])
+            x_operands[(g, c)] = (x_codes, x_scales)
+
+        def multiply(g, end):
+            for t in range(TILES):
+                if heads_done[g] == 0:
+                    acc[(g, t)] = sums.tile([P, FEAT], F32, name="acc", tag="acc")
+                for head in range(heads_done[g], end):
+                    x_codes, x_scales = x_operands[(g, head // X_HEADS)]
+                    strip = (head % X_HEADS) * TILES + t
+                    nc.tensor.matmul_mx(
+                        out=acc[(g, t)][:],
+                        lhsT=x_codes[:, strip * P : (strip + 1) * P].bitcast(FP8X4),
+                        lhsT_scale=x_scales[:, strip * P : (strip + 1) * P],
+                        rhs=w_codes[:, head * FEAT : (head + 1) * FEAT].bitcast(FP8X4),
+                        rhs_scale=w_scales[:, head * FEAT : (head + 1) * FEAT],
+                        start=(head == 0),
+                        stop=(head == HEADS - 1),
+                    )
+            heads_done[g] = end
+
+        def add_bias_to_residual(g):
+            q_plus_b = rows_pool.tile([P, TILES, FEAT], F32, bufs=2)
+            nc.vector.tensor_tensor(
+                out=q_plus_b[:],
+                in0=q_raw[g][:].rearrange("p (t n) -> p t n", t=TILES),
+                in1=bias_all[:].unsqueeze(1).to_broadcast([P, TILES, FEAT]),
+                op=ADD,
+            )
+            residual[g] = q_plus_b
+
+        def take_sums(g):
+            for t in range(TILES):
+                x = rows_pool.tile([P, FEAT], F32)
+                row_sum = stats.tile([P, 1], F32)
+                nc.vector.scalar_tensor_tensor(
+                    out=x[:], in0=acc[(g, t)][:], scalar=0.0, in1=residual[g][:, t, :], op0=ADD, op1=ADD,
+                    accum_out=row_sum[:],
+                )
+                minus_mean = stats.tile([P, 1], F32)
+                nc.gpsimd.tensor_scalar(
+                    out=minus_mean[:], in0=row_sum[:], scalar1=-1.0 / FEAT, scalar2=0.0, op0=MULT, op1=ADD
+                )
+                centred[(g, t)] = (x, minus_mean)
+
+        def scale_by_gamma(g):
+            for t in range(TILES):
+                x, minus_mean = centred[(g, t)]
+                scaled = rows_pool.tile([P, FEAT], F32)
+                nc.vector.scalar_tensor_tensor(
+                    out=scaled[:], in0=x[:], scalar=minus_mean[:], in1=gamma_all[:], op0=ADD, op1=MULT
+                )
+                centred[(g, t)] = (x, minus_mean, scaled)
+
+        def normalise_and_store(g):
+            group_rows = out_rows[g * TILES * P : (g + 1) * TILES * P, :].rearrange("(p t) n -> p t n", t=TILES)
+            for t in range(TILES):
+                x, minus_mean, scaled = centred[(g, t)]
+                squares = rows_pool.tile([P, FEAT], F32, bufs=2)
+                square_sum = stats.tile([P, 1], F32)
+                nc.scalar.activation(
+                    out=squares[:], in_=x[:], func=SQUARE, bias=minus_mean[:], scale=1.0, accum_out=square_sum[:]
+                )
+                inverse = stats.tile([P, 1], F32)
+                nc.scalar.activation(out=inverse[:], in_=square_sum[:], func=INV_SQRT, bias=eps[:], scale=1.0 / FEAT)
+                nc.vector.scalar_tensor_tensor(
+                    out=scaled[:], in0=scaled[:], scalar=inverse[:], in1=beta_all[:], op0=MULT, op1=ADD
+                )
+                nc.sync.dma_start(out=group_rows[:, t, :], in_=scaled[:])
+
+        prepare_w(0)
+        prepare_x(0, 0)
+        prepare_w(1)
+        multiply(0, W_HEADS)
+        prepare_w(2)
+        multiply(0, 2 * W_HEADS)
+        prepare_x(0, 1)
+        spread_vectors()
+        prepare_w(3)
+        multiply(0, 3 * W_HEADS)
+        add_bias_to_residual(0)
+        for g in range(1, GROUPS):
+            add_bias_to_residual(g)
+            prepare_x(g, 0)
+            multiply(g - 1, HEADS)
+            take_sums(g - 1)
+            prepare_x(g, 1)
+            scale_by_gamma(g - 1)
+            normalise_and_store(g - 1)
+            multiply(g, X_HEADS)
+        multiply(GROUPS - 1, HEADS)
+        take_sums(GROUPS - 1)
+        scale_by_gamma(GROUPS - 1)
+        normalise_and_store(GROUPS - 1)

@@ -40,6 +40,7 @@ def tile_multiheadattention_pb_kernel(tc, heads, q, proj_w, proj_b, ln_gamma, ln
         ctx.enter_context(tc.manual_schedule())
         const = ctx.enter_context(tc.tile_pool(name="const", bufs=1))
         raw = ctx.enter_context(tc.tile_pool(name="raw", bufs=1))
+        packs = ctx.enter_context(tc.tile_pool(name="packs", bufs=2))
         stage = ctx.enter_context(tc.tile_pool(name="stage", bufs=3))
         operands = ctx.enter_context(tc.tile_pool(name="operands", bufs=3))
         rows_pool = ctx.enter_context(tc.tile_pool(name="rows", bufs=4))
@@ -113,7 +114,7 @@ def tile_multiheadattention_pb_kernel(tc, heads, q, proj_w, proj_b, ln_gamma, ln
 
         def spread_vectors():
             for j, spread in enumerate((bias_all, gamma_all, beta_all)):
-                bank = banks.tile([P, FEAT], F32, tag="bank")
+                bank = sums.tile([P, FEAT], F32, name="acc", tag="acc")
                 nc.tensor.matmul(out=bank[:], lhsT=ones[:], rhs=vector_rows[:, j, :], start=True, stop=True)
                 nc.vector.tensor_copy(out=spread[:], in_=bank[:])
 
@@ -125,17 +126,29 @@ def tile_multiheadattention_pb_kernel(tc, heads, q, proj_w, proj_b, ln_gamma, ln
         residual = {}
         centred = {}
 
-        def prepare(pieces, order, codes, scales):
+        sorted_words = {}
+
+        def sort_words(key, pieces):
+            for b, copy in ((PIECES - 2, nc.scalar.copy), (PIECES - 1, nc.vector.tensor_copy)):
+                pack = packs.tile([P, BANK_STRIPS * FEAT], BF16, name="pack%d" % b)
+                copy(
+                    out=pack[:].bitcast(F32).rearrange("p (a u w) -> p a u w", a=BANK_STRIPS, u=2),
+                    in_=pieces[b][:].bitcast(F32).rearrange("p (a w u) -> p a u w", a=BANK_STRIPS, u=2),
+                )
+                sorted_words[(key, b)] = pack
+
+        def prepare(key, pieces, order, codes, scales):
             grouped = stage.tile([P, STRIPS * FEAT], BF16, align_bytes=64)
             places = grouped[:].bitcast(F32).rearrange(order, a=BANK_STRIPS, b=PIECES, u=2)
             for b in range(PIECES):
-                words = pieces[b][:].bitcast(F32)
                 bank = banks.tile([P, FEAT], F32, tag="bank")
                 for j in range(BANK_STRIPS * 2):
                     a, u = divmod(j, 2)
-                    nc.tensor.transpose(
-                        bank[:, j * P : (j + 1) * P], words[:, a * 2 * P + u : (a + 1) * 2 * P : 2], ident[:]
-                    )
+                    if (key, b) in sorted_words:
+                        picked = sorted_words[(key, b)][:].bitcast(F32)[:, j * P : (j + 1) * P]
+                    else:
+                        picked = pieces[b][:].bitcast(F32)[:, a * 2 * P + u : (a + 1) * 2 * P : 2]
+                    nc.tensor.transpose(bank[:, j * P : (j + 1) * P], picked, ident[:])
                 nc.scalar.copy(out=places[:, b, :, :, :], in_=bank[:].rearrange("p (a u r) -> p a r u", a=BANK_STRIPS, u=2))
             for s in range(0, STRIPS, QUANT_STRIPS):
                 nc.vector.quantize_mx(
@@ -146,12 +159,12 @@ def tile_multiheadattention_pb_kernel(tc, heads, q, proj_w, proj_b, ln_gamma, ln
 
         def prepare_w(c):
             columns = slice(c * STRIPS * P, (c + 1) * STRIPS * P)
-            prepare(w_raw[c], "p (a b r u) -> p b a r u", w_codes[:, columns], w_scales[:, columns])
+            prepare(("w", c), w_raw[c], "p (a b r u) -> p b a r u", w_codes[:, columns], w_scales[:, columns])
 
         def prepare_x(g, c):
             x_codes = operands.tile([P, STRIPS * P], U32, align_bytes=64)
             x_scales = operands.tile([P, STRIPS * P], U8, align_bytes=64)
-            prepare(x_raw[(g, c)], "p (b a r u) -> p b a r u", x_codes[:], x_scales[:])
+            prepare((g, c), x_raw[(g, c)], "p (b a r u) -> p b a r u", x_codes[:], x_scales[:])
             x_operands[(g, c)] = (x_codes, x_scales)
 
         def multiply(g, end):
@@ -222,22 +235,26 @@ def tile_multiheadattention_pb_kernel(tc, heads, q, proj_w, proj_b, ln_gamma, ln
                 nc.sync.dma_start(out=group_rows[:, t, :], in_=scaled[:])
 
         prepare_w(0)
+        spread_vectors()
         prepare_x(0, 0)
         prepare_w(1)
         multiply(0, W_HEADS)
         prepare_w(2)
         multiply(0, 2 * W_HEADS)
         prepare_x(0, 1)
-        spread_vectors()
         prepare_w(3)
+        sort_words((1, 0), x_raw[(1, 0)])
         multiply(0, 3 * W_HEADS)
         add_bias_to_residual(0)
         for g in range(1, GROUPS):
             add_bias_to_residual(g)
             prepare_x(g, 0)
+            sort_words((g, 1), x_raw[(g, 1)])
             multiply(g - 1, HEADS)
             take_sums(g - 1)
             prepare_x(g, 1)
+            if g + 1 < GROUPS:
+                sort_words((g + 1, 0), x_raw[(g + 1, 0)])
             scale_by_gamma(g - 1)
             normalise_and_store(g - 1)
             multiply(g, X_HEADS)

@@ -31,6 +31,10 @@ X_HEADS = STRIPS // TILES
 W_HEADS = STRIPS * P // FEAT
 
 
+def SORTERS(nc):
+    return ((PIECES - 2, nc.scalar.copy), (PIECES - 1, nc.vector.tensor_copy))
+
+
 def tile_multiheadattention_pb_kernel(tc, heads, q, proj_w, proj_b, ln_gamma, ln_beta, out):
     nc = tc.nc
     q_rows = q.flatten_outer_dims()
@@ -46,7 +50,8 @@ def tile_multiheadattention_pb_kernel(tc, heads, q, proj_w, proj_b, ln_gamma, ln
         rows_pool = ctx.enter_context(tc.tile_pool(name="rows", bufs=4))
         stats = ctx.enter_context(tc.tile_pool(name="stats", bufs=4))
         banks = ctx.enter_context(tc.psum_pool(name="banks", bufs=4))
-        sums = ctx.enter_context(tc.psum_pool(name="sums", bufs=4))
+        sums = ctx.enter_context(tc.psum_pool(name="sums", bufs=3))
+        fixed = ctx.enter_context(tc.psum_pool(name="fixed", bufs=1))
 
         ident = const.tile([P, P], F32)
         make_identity(nc, ident[:])
@@ -109,27 +114,29 @@ def tile_multiheadattention_pb_kernel(tc, heads, q, proj_w, proj_b, ln_gamma, ln
             load_x(g, 1)
 
         bias_all = const.tile([P, FEAT], F32)
-        gamma_all = const.tile([P, FEAT], F32)
-        beta_all = const.tile([P, FEAT], F32)
+        gamma_beta = fixed.tile([P, 2, FEAT], BF16)
 
         def spread_vectors():
-            for j, spread in enumerate((bias_all, gamma_all, beta_all)):
-                bank = sums.tile([P, FEAT], F32, name="acc", tag="acc")
-                nc.tensor.matmul(out=bank[:], lhsT=ones[:], rhs=vector_rows[:, j, :], start=True, stop=True)
-                nc.vector.tensor_copy(out=spread[:], in_=bank[:])
+            bank = sums.tile([P, FEAT], F32, name="acc", tag="acc")
+            nc.tensor.matmul(out=bank[:], lhsT=ones[:], rhs=vector_rows[:, 0, :], start=True, stop=True)
+            nc.vector.tensor_copy(out=bias_all[:], in_=bank[:])
+            for j in range(2):
+                nc.tensor.matmul(
+                    out=gamma_beta[:, j, :], lhsT=ones[:], rhs=vector_rows[:, 1 + j, :], start=True, stop=True
+                )
 
         w_codes = const.tile([P, HEADS * FEAT], U32, align_bytes=64)
         w_scales = const.tile([P, HEADS * FEAT], U8, align_bytes=64)
         x_operands = {}
-        heads_done = [0] * GROUPS
+        heads_done = {}
         acc = {}
         residual = {}
         centred = {}
-
         sorted_words = {}
+        chunks = {}
 
         def sort_words(key, pieces):
-            for b, copy in ((PIECES - 2, nc.scalar.copy), (PIECES - 1, nc.vector.tensor_copy)):
+            for b, copy in SORTERS(nc):
                 pack = packs.tile([P, BANK_STRIPS * FEAT], BF16, name="pack%d" % b)
                 copy(
                     out=pack[:].bitcast(F32).rearrange("p (a u w) -> p a u w", a=BANK_STRIPS, u=2),
@@ -137,11 +144,11 @@ def tile_multiheadattention_pb_kernel(tc, heads, q, proj_w, proj_b, ln_gamma, ln
                 )
                 sorted_words[(key, b)] = pack
 
-        def prepare(key, pieces, order, codes, scales):
-            grouped = stage.tile([P, STRIPS * FEAT], BF16, align_bytes=64)
-            places = grouped[:].bitcast(F32).rearrange(order, a=BANK_STRIPS, b=PIECES, u=2)
+        def transpose_chunk(key, pieces, order, codes, scales):
+            grouped = stage.tile([P, STRIPS * FEAT], BF16, name="grouped", align_bytes=64)
+            filled = []
             for b in range(PIECES):
-                bank = banks.tile([P, FEAT], F32, tag="bank")
+                bank = banks.tile([P, FEAT], F32, name="bank", tag="bank")
                 for j in range(BANK_STRIPS * 2):
                     a, u = divmod(j, 2)
                     if (key, b) in sorted_words:
@@ -149,7 +156,19 @@ def tile_multiheadattention_pb_kernel(tc, heads, q, proj_w, proj_b, ln_gamma, ln
                     else:
                         picked = pieces[b][:].bitcast(F32)[:, a * 2 * P + u : (a + 1) * 2 * P : 2]
                     nc.tensor.transpose(bank[:, j * P : (j + 1) * P], picked, ident[:])
-                nc.scalar.copy(out=places[:, b, :, :, :], in_=bank[:].rearrange("p (a u r) -> p a r u", a=BANK_STRIPS, u=2))
+                filled.append(bank)
+            chunks[key] = (grouped, filled, order, codes, scales)
+
+        def empty_banks(key, which):
+            grouped, filled, order, codes, scales = chunks[key]
+            places = grouped[:].bitcast(F32).rearrange(order, a=BANK_STRIPS, b=PIECES, u=2)
+            for b in which:
+                nc.scalar.copy(
+                    out=places[:, b, :, :, :], in_=filled[b][:].rearrange("p (a u r) -> p a r u", a=BANK_STRIPS, u=2)
+                )
+
+        def quantise(key):
+            grouped, filled, order, codes, scales = chunks[key]
             for s in range(0, STRIPS, QUANT_STRIPS):
                 nc.vector.quantize_mx(
                     out=codes[:, s * P : (s + QUANT_STRIPS) * P].bitcast(FP8X4),
@@ -157,21 +176,25 @@ def tile_multiheadattention_pb_kernel(tc, heads, q, proj_w, proj_b, ln_gamma, ln
                     in_=grouped[:, s * FEAT : (s + QUANT_STRIPS) * FEAT],
                 )
 
-        def prepare_w(c):
+        def transpose_w(c):
             columns = slice(c * STRIPS * P, (c + 1) * STRIPS * P)
-            prepare(("w", c), w_raw[c], "p (a b r u) -> p b a r u", w_codes[:, columns], w_scales[:, columns])
+            transpose_chunk(("w", c), w_raw[c], "p (a b r u) -> p b a r u", w_codes[:, columns], w_scales[:, columns])
 
-        def prepare_x(g, c):
-            x_codes = operands.tile([P, STRIPS * P], U32, align_bytes=64)
-            x_scales = operands.tile([P, STRIPS * P], U8, align_bytes=64)
-            prepare((g, c), x_raw[(g, c)], "p (b a r u) -> p b a r u", x_codes[:], x_scales[:])
+        def transpose_x(g, c):
+            x_codes = operands.tile([P, STRIPS * P], U32, name="x_codes", align_bytes=64)
+            x_scales = operands.tile([P, STRIPS * P], U8, name="x_scales", align_bytes=64)
+            transpose_chunk((g, c), x_raw[(g, c)], "p (b a r u) -> p b a r u", x_codes[:], x_scales[:])
             x_operands[(g, c)] = (x_codes, x_scales)
+
+        def prepare(key):
+            empty_banks(key, range(PIECES))
+            quantise(key)
 
         def multiply(g, end):
             for t in range(TILES):
-                if heads_done[g] == 0:
+                if (g, t) not in heads_done:
                     acc[(g, t)] = sums.tile([P, FEAT], F32, name="acc", tag="acc")
-                for head in range(heads_done[g], end):
+                for head in range(heads_done.get((g, t), 0), end):
                     x_codes, x_scales = x_operands[(g, head // X_HEADS)]
                     strip = (head % X_HEADS) * TILES + t
                     nc.tensor.matmul_mx(
@@ -183,82 +206,95 @@ def tile_multiheadattention_pb_kernel(tc, heads, q, proj_w, proj_b, ln_gamma, ln
                         start=(head == 0),
                         stop=(head == HEADS - 1),
                     )
-            heads_done[g] = end
+                heads_done[(g, t)] = end
 
         def add_bias_to_residual(g):
-            q_plus_b = rows_pool.tile([P, TILES, FEAT], F32, bufs=2)
-            nc.vector.tensor_tensor(
-                out=q_plus_b[:],
-                in0=q_raw[g][:].rearrange("p (t n) -> p t n", t=TILES),
-                in1=bias_all[:].unsqueeze(1).to_broadcast([P, TILES, FEAT]),
-                op=ADD,
-            )
+            q_plus_b = rows_pool.tile([P, TILES, FEAT], F32, name="q_plus_b", bufs=2)
+            for t in range(TILES):
+                nc.gpsimd.tensor_tensor(
+                    out=q_plus_b[:, t, :], in0=q_raw[g][:, t * FEAT : (t + 1) * FEAT], in1=bias_all[:], op=ADD
+                )
             residual[g] = q_plus_b
 
         def take_sums(g):
             for t in range(TILES):
-                x = rows_pool.tile([P, FEAT], F32)
-                row_sum = stats.tile([P, 1], F32)
+                x = rows_pool.tile([P, FEAT], F32, name="x")
+                row_sum = stats.tile([P, 1], F32, name="row_sum")
                 nc.vector.scalar_tensor_tensor(
                     out=x[:], in0=acc[(g, t)][:], scalar=0.0, in1=residual[g][:, t, :], op0=ADD, op1=ADD,
                     accum_out=row_sum[:],
                 )
-                minus_mean = stats.tile([P, 1], F32)
+                minus_mean = stats.tile([P, 1], F32, name="minus_mean")
                 nc.gpsimd.tensor_scalar(
                     out=minus_mean[:], in0=row_sum[:], scalar1=-1.0 / FEAT, scalar2=0.0, op0=MULT, op1=ADD
                 )
                 centred[(g, t)] = (x, minus_mean)
 
+        def inverse_deviation(g, t):
+            x, minus_mean, scaled = centred[(g, t)]
+            squares = rows_pool.tile([P, FEAT], F32, name="squares", bufs=2)
+            square_sum = stats.tile([P, 1], F32, name="square_sum")
+            nc.scalar.activation(
+                out=squares[:], in_=x[:], func=SQUARE, bias=minus_mean[:], scale=1.0, accum_out=square_sum[:]
+            )
+            inverse = stats.tile([P, 1], F32, name="inverse")
+            nc.scalar.activation(out=inverse[:], in_=square_sum[:], func=INV_SQRT, bias=eps[:], scale=1.0 / FEAT)
+            centred[(g, t)] = (scaled, inverse)
+
         def scale_by_gamma(g):
             for t in range(TILES):
                 x, minus_mean = centred[(g, t)]
-                scaled = rows_pool.tile([P, FEAT], F32)
+                scaled = rows_pool.tile([P, FEAT], F32, name="scaled")
                 nc.vector.scalar_tensor_tensor(
-                    out=scaled[:], in0=x[:], scalar=minus_mean[:], in1=gamma_all[:], op0=ADD, op1=MULT
+                    out=scaled[:], in0=x[:], scalar=minus_mean[:], in1=gamma_beta[:, 0, :], op0=ADD, op1=MULT
                 )
                 centred[(g, t)] = (x, minus_mean, scaled)
 
         def normalise_and_store(g):
             group_rows = out_rows[g * TILES * P : (g + 1) * TILES * P, :].rearrange("(p t) n -> p t n", t=TILES)
             for t in range(TILES):
-                x, minus_mean, scaled = centred[(g, t)]
-                squares = rows_pool.tile([P, FEAT], F32, bufs=2)
-                square_sum = stats.tile([P, 1], F32)
-                nc.scalar.activation(
-                    out=squares[:], in_=x[:], func=SQUARE, bias=minus_mean[:], scale=1.0, accum_out=square_sum[:]
-                )
-                inverse = stats.tile([P, 1], F32)
-                nc.scalar.activation(out=inverse[:], in_=square_sum[:], func=INV_SQRT, bias=eps[:], scale=1.0 / FEAT)
+                scaled, inverse = centred[(g, t)]
                 nc.vector.scalar_tensor_tensor(
-                    out=scaled[:], in0=scaled[:], scalar=inverse[:], in1=beta_all[:], op0=MULT, op1=ADD
+                    out=scaled[:], in0=scaled[:], scalar=inverse[:], in1=gamma_beta[:, 1, :], op0=MULT, op1=ADD
                 )
                 nc.sync.dma_start(out=group_rows[:, t, :], in_=scaled[:])
 
-        prepare_w(0)
+        transpose_w(0)
+        prepare(("w", 0))
         spread_vectors()
-        prepare_x(0, 0)
-        prepare_w(1)
+        transpose_x(0, 0)
+        prepare((0, 0))
+        transpose_w(1)
+        prepare(("w", 1))
         multiply(0, W_HEADS)
-        prepare_w(2)
+        transpose_w(2)
+        prepare(("w", 2))
         multiply(0, 2 * W_HEADS)
-        prepare_x(0, 1)
-        prepare_w(3)
+        transpose_x(0, 1)
+        prepare((0, 1))
+        transpose_w(3)
+        prepare(("w", 3))
         sort_words((1, 0), x_raw[(1, 0)])
         multiply(0, 3 * W_HEADS)
         add_bias_to_residual(0)
-        for g in range(1, GROUPS):
-            add_bias_to_residual(g)
-            prepare_x(g, 0)
-            sort_words((g, 1), x_raw[(g, 1)])
+        add_bias_to_residual(1)
+        for g in range(1, GROUPS + 1):
+            if g < GROUPS:
+                transpose_x(g, 0)
+                prepare((g, 0))
+                sort_words((g, 1), x_raw[(g, 1)])
             multiply(g - 1, HEADS)
             take_sums(g - 1)
-            prepare_x(g, 1)
             if g + 1 < GROUPS:
-                sort_words((g + 1, 0), x_raw[(g + 1, 0)])
+                add_bias_to_residual(g + 1)
             scale_by_gamma(g - 1)
+            if g < GROUPS:
+                transpose_x(g, 1)
+                prepare((g, 1))
+                if g + 1 < GROUPS:
+                    sort_words((g + 1, 0), x_raw[(g + 1, 0)])
+            inverse_deviation(g - 1, 0)
+            inverse_deviation(g - 1, 1)
             normalise_and_store(g - 1)
-            multiply(g, X_HEADS)
-        multiply(GROUPS - 1, HEADS)
-        take_sums(GROUPS - 1)
-        scale_by_gamma(GROUPS - 1)
-        normalise_and_store(GROUPS - 1)
+            if g < GROUPS:
+                multiply(g, X_HEADS)

@@ -31,8 +31,8 @@ X_HEADS = STRIPS // TILES
 W_HEADS = STRIPS * P // FEAT
 
 
-def SORTERS(nc):
-    return ((PIECES - 2, nc.scalar.copy), (PIECES - 1, nc.vector.tensor_copy))
+VECTOR_SORTS = (1, 3)
+SCALAR_SORTS = (2,)
 
 
 def tile_multiheadattention_pb_kernel(tc, heads, q, proj_w, proj_b, ln_gamma, ln_beta, out):
@@ -135,8 +135,9 @@ def tile_multiheadattention_pb_kernel(tc, heads, q, proj_w, proj_b, ln_gamma, ln
         sorted_words = {}
         chunks = {}
 
-        def sort_words(key, pieces):
-            for b, copy in SORTERS(nc):
+        def sort_words(key, which, copy):
+            pieces = x_raw[key]
+            for b in which:
                 pack = packs.tile([P, BANK_STRIPS * FEAT], BF16, name="pack%d" % b)
                 copy(
                     out=pack[:].bitcast(F32).rearrange("p (a u w) -> p a u w", a=BANK_STRIPS, u=2),
@@ -273,16 +274,18 @@ def tile_multiheadattention_pb_kernel(tc, heads, q, proj_w, proj_b, ln_gamma, ln
         transpose_x(0, 1)
         prepare((0, 1))
         transpose_w(3)
+        sort_words((1, 0), VECTOR_SORTS, nc.vector.tensor_copy)
         prepare(("w", 3))
-        sort_words((1, 0), x_raw[(1, 0)])
+        sort_words((1, 0), SCALAR_SORTS, nc.scalar.copy)
         multiply(0, 3 * W_HEADS)
         add_bias_to_residual(0)
         add_bias_to_residual(1)
         for g in range(1, GROUPS + 1):
             if g < GROUPS:
                 transpose_x(g, 0)
+                sort_words((g, 1), VECTOR_SORTS, nc.vector.tensor_copy)
                 prepare((g, 0))
-                sort_words((g, 1), x_raw[(g, 1)])
+                sort_words((g, 1), SCALAR_SORTS, nc.scalar.copy)
             multiply(g - 1, HEADS)
             take_sums(g - 1)
             if g + 1 < GROUPS:
@@ -290,9 +293,11 @@ def tile_multiheadattention_pb_kernel(tc, heads, q, proj_w, proj_b, ln_gamma, ln
             scale_by_gamma(g - 1)
             if g < GROUPS:
                 transpose_x(g, 1)
+                if g + 1 < GROUPS:
+                    sort_words((g + 1, 0), VECTOR_SORTS, nc.vector.tensor_copy)
                 prepare((g, 1))
                 if g + 1 < GROUPS:
-                    sort_words((g + 1, 0), x_raw[(g + 1, 0)])
+                    sort_words((g + 1, 0), SCALAR_SORTS, nc.scalar.copy)
             inverse_deviation(g - 1, 0)
             inverse_deviation(g - 1, 1)
             normalise_and_store(g - 1)

@@ -70,27 +70,32 @@ def tile_multiheadattention_pb_kernel(tc, heads, q, proj_w, proj_b, ln_gamma, ln
         x_raw = {}
         q_raw = []
 
-        def load_w(c):
+        def load_w(c, together):
             pieces = []
-            for b in range(PIECES):
-                piece = raw.tile([P, BANK_STRIPS * FEAT], BF16, name="w_raw%d_%d" % (c, b))
+            for b in range(0, PIECES, together):
+                several = raw.tile([P, together, BANK_STRIPS * FEAT], BF16, name="w_raw%d_%d" % (c, b))
                 nc.sync.dma_start(
-                    out=piece[:], in_=proj_w[b * P : (b + 1) * P, c * W_HEADS * FEAT : (c + 1) * W_HEADS * FEAT]
-                )
-                pieces.append(piece)
-            w_raw.append(pieces)
-
-        def load_x(g, c):
-            pieces = []
-            for b in range(PIECES):
-                piece = raw.tile([P, BANK_STRIPS * FEAT], BF16, name="x_raw%d_%d_%d" % (g, c, b))
-                nc.sync.dma_start(
-                    out=piece[:],
-                    in_=heads[c * X_HEADS + b, g * TILES * P : (g + 1) * TILES * P, :].rearrange(
-                        "(p t) d -> p (t d)", t=TILES
+                    out=several[:],
+                    in_=proj_w[b * P : (b + together) * P, c * W_HEADS * FEAT : (c + 1) * W_HEADS * FEAT].rearrange(
+                        "(b p) k -> p b k", b=together
                     ),
                 )
-                pieces.append(piece)
+                for j in range(together):
+                    pieces.append(several[:, j, :])
+            w_raw.append(pieces)
+
+        def load_x(g, c, together):
+            pieces = []
+            for b in range(0, PIECES, together):
+                several = raw.tile([P, together, BANK_STRIPS * FEAT], BF16, name="x_raw%d_%d_%d" % (g, c, b))
+                nc.sync.dma_start(
+                    out=several[:],
+                    in_=heads[
+                        c * X_HEADS + b : c * X_HEADS + b + together, g * TILES * P : (g + 1) * TILES * P, :
+                    ].rearrange("h (p t) d -> p h (t d)", t=TILES),
+                )
+                for j in range(together):
+                    pieces.append(several[:, j, :])
             x_raw[(g, c)] = pieces
 
         def load_q(g):
@@ -101,17 +106,17 @@ def tile_multiheadattention_pb_kernel(tc, heads, q, proj_w, proj_b, ln_gamma, ln
             )
             q_raw.append(q_group)
 
-        load_w(0)
-        load_x(0, 0)
-        load_w(1)
-        load_w(2)
-        load_x(0, 1)
-        load_w(3)
+        load_w(0, 1)
+        load_x(0, 0, 2)
+        load_w(1, 2)
+        load_w(2, 2)
+        load_x(0, 1, 2)
+        load_w(3, 2)
         load_q(0)
         for g in range(1, GROUPS):
+            load_x(g, 0, 2)
+            load_x(g, 1, 2)
             load_q(g)
-            load_x(g, 0)
-            load_x(g, 1)
 
         bias_all = const.tile([P, FEAT], F32)
         gamma_beta = fixed.tile([P, 2, FEAT], BF16)
@@ -136,12 +141,12 @@ def tile_multiheadattention_pb_kernel(tc, heads, q, proj_w, proj_b, ln_gamma, ln
         chunks = {}
 
         def sort_words(key, which, copy):
-            pieces = x_raw[key]
+            pieces = w_raw[key[1]] if key[0] == "w" else x_raw[key]
             for b in which:
                 pack = packs.tile([P, BANK_STRIPS * FEAT], BF16, name="pack%d" % b)
                 copy(
                     out=pack[:].bitcast(F32).rearrange("p (a u w) -> p a u w", a=BANK_STRIPS, u=2),
-                    in_=pieces[b][:].bitcast(F32).rearrange("p (a w u) -> p a u w", a=BANK_STRIPS, u=2),
+                    in_=pieces[b].bitcast(F32).rearrange("p (a w u) -> p a u w", a=BANK_STRIPS, u=2),
                 )
                 sorted_words[(key, b)] = pack
 
@@ -155,7 +160,7 @@ def tile_multiheadattention_pb_kernel(tc, heads, q, proj_w, proj_b, ln_gamma, ln
                     if (key, b) in sorted_words:
                         picked = sorted_words[(key, b)][:].bitcast(F32)[:, j * P : (j + 1) * P]
                     else:
-                        picked = pieces[b][:].bitcast(F32)[:, a * 2 * P + u : (a + 1) * 2 * P : 2]
+                        picked = pieces[b].bitcast(F32)[:, a * 2 * P + u : (a + 1) * 2 * P : 2]
                     nc.tensor.transpose(bank[:, j * P : (j + 1) * P], picked, ident[:])
                 filled.append(bank)
             chunks[key] = (grouped, filled, order, codes, scales)
@@ -266,20 +271,25 @@ def tile_multiheadattention_pb_kernel(tc, heads, q, proj_w, proj_b, ln_gamma, ln
         transpose_x(0, 0)
         prepare((0, 0))
         transpose_w(1)
+        sort_words(("w", 2), VECTOR_SORTS, nc.vector.tensor_copy)
         prepare(("w", 1))
+        sort_words(("w", 2), SCALAR_SORTS, nc.scalar.copy)
         multiply(0, W_HEADS)
         transpose_w(2)
+        sort_words((0, 1), VECTOR_SORTS, nc.vector.tensor_copy)
         prepare(("w", 2))
+        sort_words((0, 1), SCALAR_SORTS, nc.scalar.copy)
         multiply(0, 2 * W_HEADS)
         transpose_x(0, 1)
+        sort_words(("w", 3), VECTOR_SORTS, nc.vector.tensor_copy)
         prepare((0, 1))
+        sort_words(("w", 3), SCALAR_SORTS, nc.scalar.copy)
         transpose_w(3)
         sort_words((1, 0), VECTOR_SORTS, nc.vector.tensor_copy)
         prepare(("w", 3))
         sort_words((1, 0), SCALAR_SORTS, nc.scalar.copy)
         multiply(0, 3 * W_HEADS)
         add_bias_to_residual(0)
-        add_bias_to_residual(1)
         for g in range(1, GROUPS + 1):
             if g < GROUPS:
                 transpose_x(g, 0)
@@ -288,8 +298,8 @@ def tile_multiheadattention_pb_kernel(tc, heads, q, proj_w, proj_b, ln_gamma, ln
                 sort_words((g, 1), SCALAR_SORTS, nc.scalar.copy)
             multiply(g - 1, HEADS)
             take_sums(g - 1)
-            if g + 1 < GROUPS:
-                add_bias_to_residual(g + 1)
+            if g < GROUPS:
+                add_bias_to_residual(g)
             scale_by_gamma(g - 1)
             if g < GROUPS:
                 transpose_x(g, 1)

@@ -33,6 +33,7 @@ W_HEADS = STRIPS * P // FEAT
 
 VECTOR_SORTS = (1, 3)
 SCALAR_SORTS = (2,)
+EARLY_SORTS = (1, 2, 3)
 
 
 def tile_multiheadattention_pb_kernel(tc, heads, q, proj_w, proj_b, ln_gamma, ln_beta, out):
@@ -59,12 +60,12 @@ def tile_multiheadattention_pb_kernel(tc, heads, q, proj_w, proj_b, ln_gamma, ln
         nc.vector.memset(ones[:], 1.0)
         eps = const.tile([P, 1], F32)
         nc.vector.memset(eps[:], LN_EPS)
-        vector_rows = const.tile([P, 3, FEAT], BF16)
-        nc.vector.memset(vector_rows[:], 0.0)
-        for j, vector in enumerate((proj_b, ln_gamma, ln_beta)):
-            nc.scalar.dma_start(out=vector_rows[0:1, j, :], in_=vector.rearrange("(o n) -> o n", o=1))
         warm = const.tile([P, 1], F32)
         nc.scalar.activation(out=warm[:], in_=eps[:], func=INV_SQRT)
+        vector_rows = const.tile([P, 3, FEAT], BF16)
+        nc.vector.memset(vector_rows[:].rearrange("p j n -> p (j n)").bitcast(F32), 0.0)
+        for j, vector in enumerate((proj_b, ln_gamma, ln_beta)):
+            nc.scalar.dma_start(out=vector_rows[0:1, j, :], in_=vector.rearrange("(o n) -> o n", o=1))
 
         w_raw = []
         x_raw = {}
@@ -271,19 +272,16 @@ def tile_multiheadattention_pb_kernel(tc, heads, q, proj_w, proj_b, ln_gamma, ln
         transpose_x(0, 0)
         prepare((0, 0))
         transpose_w(1)
-        sort_words(("w", 2), VECTOR_SORTS, nc.vector.tensor_copy)
+        sort_words(("w", 2), EARLY_SORTS, nc.vector.tensor_copy)
         prepare(("w", 1))
-        sort_words(("w", 2), SCALAR_SORTS, nc.scalar.copy)
         multiply(0, W_HEADS)
         transpose_w(2)
-        sort_words((0, 1), VECTOR_SORTS, nc.vector.tensor_copy)
+        sort_words((0, 1), EARLY_SORTS, nc.vector.tensor_copy)
         prepare(("w", 2))
-        sort_words((0, 1), SCALAR_SORTS, nc.scalar.copy)
         multiply(0, 2 * W_HEADS)
         transpose_x(0, 1)
-        sort_words(("w", 3), VECTOR_SORTS, nc.vector.tensor_copy)
+        sort_words(("w", 3), EARLY_SORTS, nc.vector.tensor_copy)
         prepare((0, 1))
-        sort_words(("w", 3), SCALAR_SORTS, nc.scalar.copy)
         transpose_w(3)
         sort_words((1, 0), VECTOR_SORTS, nc.vector.tensor_copy)
         prepare(("w", 3))

@@ -235,36 +235,43 @@ def tile_multiheadattention_pb_kernel(tc, heads, q, proj_w, proj_b, ln_gamma, ln
                 nc.gpsimd.tensor_scalar(
                     out=minus_mean[:], in0=row_sum[:], scalar1=-1.0 / FEAT, scalar2=0.0, op0=MULT, op1=ADD
                 )
-                centred[(g, t)] = (x, minus_mean)
+                centred[(g, t)] = (x, row_sum, minus_mean)
 
         def inverse_deviation(g, t):
-            x, minus_mean, scaled = centred[(g, t)]
+            x, row_sum, scaled = centred[(g, t)]
             squares = rows_pool.tile([P, FEAT], F32, name="squares", bufs=2)
             square_sum = stats.tile([P, 1], F32, name="square_sum")
             nc.scalar.activation(
-                out=squares[:], in_=x[:], func=SQUARE, bias=minus_mean[:], scale=1.0, accum_out=square_sum[:]
+                out=squares[:], in_=x[:], func=SQUARE, bias=row_sum[:], scale=-1.0 * FEAT, accum_out=square_sum[:]
             )
             inverse = stats.tile([P, 1], F32, name="inverse")
-            nc.scalar.activation(out=inverse[:], in_=square_sum[:], func=INV_SQRT, bias=eps[:], scale=1.0 / FEAT)
+            nc.scalar.activation(
+                out=inverse[:], in_=square_sum[:], func=INV_SQRT, bias=eps[:], scale=1.0 / (FEAT * FEAT * FEAT)
+            )
             centred[(g, t)] = (scaled, inverse)
 
         def scale_by_gamma(g):
             for t in range(TILES):
-                x, minus_mean = centred[(g, t)]
+                x, row_sum, minus_mean = centred[(g, t)]
                 scaled = rows_pool.tile([P, FEAT], F32, name="scaled")
                 nc.vector.scalar_tensor_tensor(
                     out=scaled[:], in0=x[:], scalar=minus_mean[:], in1=gamma_beta[:, 0, :], op0=ADD, op1=MULT
                 )
-                centred[(g, t)] = (x, minus_mean, scaled)
+                centred[(g, t)] = (x, row_sum, scaled)
 
         def normalise_and_store(g):
             group_rows = out_rows[g * TILES * P : (g + 1) * TILES * P, :].rearrange("(p t) n -> p t n", t=TILES)
             for t in range(TILES):
                 scaled, inverse = centred[(g, t)]
-                nc.vector.scalar_tensor_tensor(
-                    out=scaled[:], in0=scaled[:], scalar=inverse[:], in1=gamma_beta[:, 1, :], op0=MULT, op1=ADD
-                )
-                nc.sync.dma_start(out=group_rows[:, t, :], in_=scaled[:])
+                parts = 2 if (g == GROUPS - 1 and t == TILES - 1) else 1
+                width = FEAT // parts
+                for i in range(parts):
+                    columns = slice(i * width, (i + 1) * width)
+                    nc.vector.scalar_tensor_tensor(
+                        out=scaled[:, columns], in0=scaled[:, columns], scalar=inverse[:],
+                        in1=gamma_beta[:, 1, columns], op0=MULT, op1=ADD,
+                    )
+                    nc.sync.dma_start(out=group_rows[:, t, columns], in_=scaled[:, columns])
 
         transpose_w(0)
         prepare(("w", 0))

@@ -138,6 +138,8 @@ def tile_multiheadattention_pb_kernel(tc, heads, q, proj_w, proj_b, ln_gamma, ln
         acc = {}
         residual = {}
         centred = {}
+        inverses = {}
+        scaled_rows = {}
         sorted_words = {}
         chunks = {}
 
@@ -174,9 +176,9 @@ def tile_multiheadattention_pb_kernel(tc, heads, q, proj_w, proj_b, ln_gamma, ln
                     out=places[:, b, :, :, :], in_=filled[b][:].rearrange("p (a u r) -> p a r u", a=BANK_STRIPS, u=2)
                 )
 
-        def quantise(key):
+        def quantise(key, halves=(0, 1)):
             grouped, filled, order, codes, scales = chunks[key]
-            for s in range(0, STRIPS, QUANT_STRIPS):
+            for s in (half * QUANT_STRIPS for half in halves):
                 nc.vector.quantize_mx(
                     out=codes[:, s * P : (s + QUANT_STRIPS) * P].bitcast(FP8X4),
                     scales=scales[:, s * P : (s + QUANT_STRIPS) * P],
@@ -197,48 +199,49 @@ def tile_multiheadattention_pb_kernel(tc, heads, q, proj_w, proj_b, ln_gamma, ln
             empty_banks(key, range(PIECES))
             quantise(key)
 
+        def multiply_tile(g, t, end):
+            if (g, t) not in heads_done:
+                acc[(g, t)] = sums.tile([P, FEAT], F32, name="acc", tag="acc")
+            for head in range(heads_done.get((g, t), 0), end):
+                x_codes, x_scales = x_operands[(g, head // X_HEADS)]
+                strip = (head % X_HEADS) * TILES + t
+                nc.tensor.matmul_mx(
+                    out=acc[(g, t)][:],
+                    lhsT=x_codes[:, strip * P : (strip + 1) * P].bitcast(FP8X4),
+                    lhsT_scale=x_scales[:, strip * P : (strip + 1) * P],
+                    rhs=w_codes[:, head * FEAT : (head + 1) * FEAT].bitcast(FP8X4),
+                    rhs_scale=w_scales[:, head * FEAT : (head + 1) * FEAT],
+                    start=(head == 0),
+                    stop=(head == HEADS - 1),
+                )
+            heads_done[(g, t)] = end
+
         def multiply(g, end):
             for t in range(TILES):
-                if (g, t) not in heads_done:
-                    acc[(g, t)] = sums.tile([P, FEAT], F32, name="acc", tag="acc")
-                for head in range(heads_done.get((g, t), 0), end):
-                    x_codes, x_scales = x_operands[(g, head // X_HEADS)]
-                    strip = (head % X_HEADS) * TILES + t
-                    nc.tensor.matmul_mx(
-                        out=acc[(g, t)][:],
-                        lhsT=x_codes[:, strip * P : (strip + 1) * P].bitcast(FP8X4),
-                        lhsT_scale=x_scales[:, strip * P : (strip + 1) * P],
-                        rhs=w_codes[:, head * FEAT : (head + 1) * FEAT].bitcast(FP8X4),
-                        rhs_scale=w_scales[:, head * FEAT : (head + 1) * FEAT],
-                        start=(head == 0),
-                        stop=(head == HEADS - 1),
-                    )
-                heads_done[(g, t)] = end
+                multiply_tile(g, t, end)
 
-        def add_bias_to_residual(g):
-            q_plus_b = rows_pool.tile([P, TILES, FEAT], F32, name="q_plus_b", bufs=2)
-            for t in range(TILES):
-                nc.gpsimd.tensor_tensor(
-                    out=q_plus_b[:, t, :], in0=q_raw[g][:, t * FEAT : (t + 1) * FEAT], in1=bias_all[:], op=ADD
-                )
-            residual[g] = q_plus_b
+        def add_bias_to_residual(g, t):
+            q_plus_b = rows_pool.tile([P, FEAT], F32, name="q_plus_b")
+            nc.gpsimd.tensor_tensor(
+                out=q_plus_b[:], in0=q_raw[g][:, t * FEAT : (t + 1) * FEAT], in1=bias_all[:], op=ADD
+            )
+            residual[(g, t)] = q_plus_b
 
-        def take_sums(g):
-            for t in range(TILES):
-                x = rows_pool.tile([P, FEAT], F32, name="x")
-                row_sum = stats.tile([P, 1], F32, name="row_sum")
-                nc.vector.scalar_tensor_tensor(
-                    out=x[:], in0=acc[(g, t)][:], scalar=0.0, in1=residual[g][:, t, :], op0=ADD, op1=ADD,
-                    accum_out=row_sum[:],
-                )
-                minus_mean = stats.tile([P, 1], F32, name="minus_mean")
-                nc.gpsimd.tensor_scalar(
-                    out=minus_mean[:], in0=row_sum[:], scalar1=-1.0 / FEAT, scalar2=0.0, op0=MULT, op1=ADD
-                )
-                centred[(g, t)] = (x, row_sum, minus_mean)
+        def take_sums(g, t):
+            x = rows_pool.tile([P, FEAT], F32, name="x")
+            row_sum = stats.tile([P, 1], F32, name="row_sum")
+            nc.vector.scalar_tensor_tensor(
+                out=x[:], in0=acc[(g, t)][:], scalar=0.0, in1=residual[(g, t)][:], op0=ADD, op1=ADD,
+                accum_out=row_sum[:],
+            )
+            minus_mean = stats.tile([P, 1], F32, name="minus_mean")
+            nc.gpsimd.tensor_scalar(
+                out=minus_mean[:], in0=row_sum[:], scalar1=-1.0 / FEAT, scalar2=0.0, op0=MULT, op1=ADD
+            )
+            centred[(g, t)] = (x, row_sum, minus_mean)
 
         def inverse_deviation(g, t):
-            x, row_sum, scaled = centred[(g, t)]
+            x, row_sum, minus_mean = centred[(g, t)]
             squares = rows_pool.tile([P, FEAT], F32, name="squares", bufs=2)
             square_sum = stats.tile([P, 1], F32, name="square_sum")
             nc.scalar.activation(
@@ -248,21 +251,20 @@ def tile_multiheadattention_pb_kernel(tc, heads, q, proj_w, proj_b, ln_gamma, ln
             nc.scalar.activation(
                 out=inverse[:], in_=square_sum[:], func=INV_SQRT, bias=eps[:], scale=1.0 / (FEAT * FEAT * FEAT)
             )
-            centred[(g, t)] = (scaled, inverse)
+            inverses[(g, t)] = inverse
 
-        def scale_by_gamma(g):
-            for t in range(TILES):
-                x, row_sum, minus_mean = centred[(g, t)]
-                scaled = rows_pool.tile([P, FEAT], F32, name="scaled")
-                nc.vector.scalar_tensor_tensor(
-                    out=scaled[:], in0=x[:], scalar=minus_mean[:], in1=gamma_beta[:, 0, :], op0=ADD, op1=MULT
-                )
-                centred[(g, t)] = (x, row_sum, scaled)
+        def scale_by_gamma(g, t):
+            x, row_sum, minus_mean = centred[(g, t)]
+            scaled = rows_pool.tile([P, FEAT], F32, name="scaled")
+            nc.vector.scalar_tensor_tensor(
+                out=scaled[:], in0=x[:], scalar=minus_mean[:], in1=gamma_beta[:, 0, :], op0=ADD, op1=MULT
+            )
+            scaled_rows[(g, t)] = scaled
 
         def normalise_and_store(g):
             group_rows = out_rows[g * TILES * P : (g + 1) * TILES * P, :].rearrange("(p t) n -> p t n", t=TILES)
             for t in range(TILES):
-                scaled, inverse = centred[(g, t)]
+                scaled, inverse = scaled_rows[(g, t)], inverses[(g, t)]
                 parts = 2 if (g == GROUPS - 1 and t == TILES - 1) else 1
                 width = FEAT // parts
                 for i in range(parts):
@@ -285,8 +287,9 @@ def tile_multiheadattention_pb_kernel(tc, heads, q, proj_w, proj_b, ln_gamma, ln
         transpose_w(2)
         sort_words((0, 1), EARLY_SORTS, nc.vector.tensor_copy)
         prepare(("w", 2))
-        multiply(0, 2 * W_HEADS)
+        multiply_tile(0, 0, 2 * W_HEADS)
         transpose_x(0, 1)
+        multiply_tile(0, 1, 2 * W_HEADS)
         sort_words(("w", 3), EARLY_SORTS, nc.vector.tensor_copy)
         prepare((0, 1))
         transpose_w(3)
@@ -294,27 +297,41 @@ def tile_multiheadattention_pb_kernel(tc, heads, q, proj_w, proj_b, ln_gamma, ln
         prepare(("w", 3))
         sort_words((1, 0), SCALAR_SORTS, nc.scalar.copy)
         multiply(0, 3 * W_HEADS)
-        add_bias_to_residual(0)
-        for g in range(1, GROUPS + 1):
-            if g < GROUPS:
-                transpose_x(g, 0)
-                sort_words((g, 1), VECTOR_SORTS, nc.vector.tensor_copy)
-                prepare((g, 0))
-                sort_words((g, 1), SCALAR_SORTS, nc.scalar.copy)
-            multiply(g - 1, HEADS)
-            take_sums(g - 1)
-            if g < GROUPS:
-                add_bias_to_residual(g)
-            scale_by_gamma(g - 1)
-            if g < GROUPS:
-                transpose_x(g, 1)
-                if g + 1 < GROUPS:
-                    sort_words((g + 1, 0), VECTOR_SORTS, nc.vector.tensor_copy)
-                prepare((g, 1))
-                if g + 1 < GROUPS:
-                    sort_words((g + 1, 0), SCALAR_SORTS, nc.scalar.copy)
-            inverse_deviation(g - 1, 0)
-            inverse_deviation(g - 1, 1)
-            normalise_and_store(g - 1)
-            if g < GROUPS:
-                multiply(g, X_HEADS)
+        for t in range(TILES):
+            add_bias_to_residual(0, t)
+        for g in range(1, GROUPS):
+            before = g - 1
+            transpose_x(g, 0)
+            sort_words((g, 1), VECTOR_SORTS, nc.vector.tensor_copy)
+            empty_banks((g, 0), range(PIECES - 1))
+            sort_words((g, 1), SCALAR_SORTS, nc.scalar.copy)
+            empty_banks((g, 0), (PIECES - 1,))
+            quantise((g, 0), (0,))
+            multiply(before, HEADS)
+            add_bias_to_residual(g, 0)
+            take_sums(before, 0)
+            quantise((g, 0), (1,))
+            add_bias_to_residual(g, 1)
+            take_sums(before, 1)
+            scale_by_gamma(before, 0)
+            transpose_x(g, 1)
+            if g + 1 < GROUPS:
+                sort_words((g + 1, 0), VECTOR_SORTS, nc.vector.tensor_copy)
+                empty_banks((g, 1), range(PIECES - 1))
+                sort_words((g + 1, 0), SCALAR_SORTS, nc.scalar.copy)
+                empty_banks((g, 1), (PIECES - 1,))
+            else:
+                empty_banks((g, 1), range(PIECES))
+            quantise((g, 1))
+            scale_by_gamma(before, 1)
+            for t in range(TILES):
+                inverse_deviation(before, t)
+            normalise_and_store(before)
+            multiply(g, X_HEADS)
+        multiply(g, HEADS)
+        for t in range(TILES):
+            take_sums(g, t)
+        for t in range(TILES):
+            scale_by_gamma(g, t)
+            inverse_deviation(g, t)
+        normalise_and_store(g)

@@ -16,6 +16,7 @@ SQUARE = mybir.ActivationFunctionType.Square
 INV_SQRT = mybir.ActivationFunctionType.Abs_reciprocal_sqrt
 
 P = 128
+WINDOW = 256
 HEADS = 8
 ROWS = 1024
 FEAT = 512
@@ -131,8 +132,10 @@ def tile_multiheadattention_pb_kernel(tc, heads, q, proj_w, proj_b, ln_gamma, ln
                     out=gamma_beta[:, j, :], lhsT=ones[:], rhs=vector_rows[:, 1 + j, :], start=True, stop=True
                 )
 
-        w_codes = const.tile([P, HEADS * FEAT], U32, align_bytes=64)
-        w_scales = const.tile([P, HEADS * FEAT], U8, align_bytes=64)
+        w_codes_tile = const.tile([P, WINDOW // 4 + HEADS * FEAT], U32, name="w_codes", align_bytes=64)
+        w_codes = w_codes_tile[:, 0 // 4 : 0 // 4 + HEADS * FEAT]
+        w_scales_tile = const.tile([P, WINDOW + HEADS * FEAT], U8, name="w_scales", align_bytes=64)
+        w_scales = w_scales_tile[:, 64 : 64 + HEADS * FEAT]
         x_operands = {}
         heads_done = {}
         acc = {}
@@ -190,9 +193,11 @@ def tile_multiheadattention_pb_kernel(tc, heads, q, proj_w, proj_b, ln_gamma, ln
             transpose_chunk(("w", c), w_raw[c], "p (a b r u) -> p b a r u", w_codes[:, columns], w_scales[:, columns])
 
         def transpose_x(g, c):
-            x_codes = operands.tile([P, STRIPS * P], U32, name="x_codes", align_bytes=64)
-            x_scales = operands.tile([P, STRIPS * P], U8, name="x_scales", align_bytes=64)
-            transpose_chunk((g, c), x_raw[(g, c)], "p (b a r u) -> p b a r u", x_codes[:], x_scales[:])
+            x_codes_tile = operands.tile([P, WINDOW // 4 + STRIPS * P], U32, name="x_codes", align_bytes=64)
+            x_scales_tile = operands.tile([P, WINDOW + STRIPS * P], U8, name="x_scales", align_bytes=64)
+            x_codes = x_codes_tile[:, 128 // 4 : 128 // 4 + STRIPS * P]
+            x_scales = x_scales_tile[:, 192 : 192 + STRIPS * P]
+            transpose_chunk((g, c), x_raw[(g, c)], "p (b a r u) -> p b a r u", x_codes, x_scales)
             x_operands[(g, c)] = (x_codes, x_scales)
 
         def prepare(key):

from contextlib import ExitStack

import concourse.mybir as mybir
from concourse.masks import make_identity

FLOPS = 2 * 1024 * 4096 * 512

F32 = mybir.dt.float32
BF16 = mybir.dt.bfloat16
U32 = mybir.dt.uint32
U8 = mybir.dt.uint8
FP8X4 = mybir.dt.float8_e4m3fn_x4
ADD = mybir.AluOpType.add
MULT = mybir.AluOpType.mult
SQUARE = mybir.ActivationFunctionType.Square
INV_SQRT = mybir.ActivationFunctionType.Abs_reciprocal_sqrt

P = 128
WINDOW = 256
HEADS = 8
ROWS = 1024
FEAT = 512
LN_EPS = 1e-5

STRIPS = 8
BANK_STRIPS = 2
PIECES = STRIPS // BANK_STRIPS
QUANT_STRIPS = 4
TILES = 2
GROUPS = ROWS // (TILES * P)
X_HEADS = STRIPS // TILES
W_HEADS = STRIPS * P // FEAT


VECTOR_SORTS = (1, 3)
SCALAR_SORTS = (2,)
EARLY_SORTS = (1, 2, 3)


def tile_multiheadattention_pb_kernel(tc, heads, q, proj_w, proj_b, ln_gamma, ln_beta, out):
    nc = tc.nc
    q_rows = q.flatten_outer_dims()
    out_rows = out.flatten_outer_dims()

    with ExitStack() as ctx:
        ctx.enter_context(tc.manual_schedule())
        const = ctx.enter_context(tc.tile_pool(name="const", bufs=1))
        raw = ctx.enter_context(tc.tile_pool(name="raw", bufs=1))
        packs = ctx.enter_context(tc.tile_pool(name="packs", bufs=2))
        stage = ctx.enter_context(tc.tile_pool(name="stage", bufs=3))
        operands = ctx.enter_context(tc.tile_pool(name="operands", bufs=3))
        rows_pool = ctx.enter_context(tc.tile_pool(name="rows", bufs=4))
        stats = ctx.enter_context(tc.tile_pool(name="stats", bufs=4))
        banks = ctx.enter_context(tc.psum_pool(name="banks", bufs=4))
        sums = ctx.enter_context(tc.psum_pool(name="sums", bufs=3))
        fixed = ctx.enter_context(tc.psum_pool(name="fixed", bufs=1))

        ident = const.tile([P, P], F32)
        make_identity(nc, ident[:])
        ones = const.tile([P, P], BF16)
        nc.vector.memset(ones[:], 1.0)
        eps = const.tile([P, 1], F32)
        nc.vector.memset(eps[:], LN_EPS)
        warm = const.tile([P, 1], F32)
        nc.scalar.activation(out=warm[:], in_=eps[:], func=INV_SQRT)
        vector_rows = const.tile([P, 3, FEAT], BF16)
        nc.vector.memset(vector_rows[:].rearrange("p j n -> p (j n)").bitcast(F32), 0.0)
        for j, vector in enumerate((proj_b, ln_gamma, ln_beta)):
            nc.scalar.dma_start(out=vector_rows[0:1, j, :], in_=vector.rearrange("(o n) -> o n", o=1))

        w_raw = []
        x_raw = {}
        q_raw = []

        def load_w(c, together):
            pieces = []
            for b in range(0, PIECES, together):
                several = raw.tile([P, together, BANK_STRIPS * FEAT], BF16, name="w_raw%d_%d" % (c, b))
                nc.sync.dma_start(
                    out=several[:],
                    in_=proj_w[b * P : (b + together) * P, c * W_HEADS * FEAT : (c + 1) * W_HEADS * FEAT].rearrange(
                        "(b p) k -> p b k", b=together
                    ),
                )
                for j in range(together):
                    pieces.append(several[:, j, :])
            w_raw.append(pieces)

        def load_x(g, c, together):
            pieces = []
            for b in range(0, PIECES, together):
                several = raw.tile([P, together, BANK_STRIPS * FEAT], BF16, name="x_raw%d_%d_%d" % (g, c, b))
                nc.sync.dma_start(
                    out=several[:],
                    in_=heads[
                        c * X_HEADS + b : c * X_HEADS + b + together, g * TILES * P : (g + 1) * TILES * P, :
                    ].rearrange("h (p t) d -> p h (t d)", t=TILES),
                )
                for j in range(together):
                    pieces.append(several[:, j, :])
            x_raw[(g, c)] = pieces

        def load_q(g):
            q_group = raw.tile([P, TILES * FEAT], BF16, name="q_raw%d" % g)
            nc.sync.dma_start(
                out=q_group[:],
                in_=q_rows[g * TILES * P : (g + 1) * TILES * P, :].rearrange("(p t) n -> p (t n)", t=TILES),
            )
            q_raw.append(q_group)

        load_w(0, 1)
        load_x(0, 0, 2)
        load_w(1, 2)
        load_w(2, 2)
        load_x(0, 1, 2)
        load_w(3, 2)
        load_q(0)
        for g in range(1, GROUPS):
            load_x(g, 0, 2)
            load_x(g, 1, 2)
            load_q(g)

        bias_all = const.tile([P, FEAT], F32)
        gamma_beta = fixed.tile([P, 2, FEAT], BF16)

        def spread_vectors():
            bank = sums.tile([P, FEAT], F32, name="acc", tag="acc")
            nc.tensor.matmul(out=bank[:], lhsT=ones[:], rhs=vector_rows[:, 0, :], start=True, stop=True)
            nc.vector.tensor_copy(out=bias_all[:], in_=bank[:])
            for j in range(2):
                nc.tensor.matmul(
                    out=gamma_beta[:, j, :], lhsT=ones[:], rhs=vector_rows[:, 1 + j, :], start=True, stop=True
                )

        w_codes_tile = const.tile([P, WINDOW // 4 + HEADS * FEAT], U32, name="w_codes", align_bytes=64)
        w_codes = w_codes_tile[:, 0 // 4 : 0 // 4 + HEADS * FEAT]
        w_scales_tile = const.tile([P, WINDOW + HEADS * FEAT], U8, name="w_scales", align_bytes=64)
        w_scales = w_scales_tile[:, 64 : 64 + HEADS * FEAT]
        x_operands = {}
        heads_done = {}
        acc = {}
        residual = {}
        centred = {}
        inverses = {}
        scaled_rows = {}
        sorted_words = {}
        chunks = {}

        def sort_words(key, which, copy):
            pieces = w_raw[key[1]] if key[0] == "w" else x_raw[key]
            for b in which:
                pack = packs.tile([P, BANK_STRIPS * FEAT], BF16, name="pack%d" % b)
                copy(
                    out=pack[:].bitcast(F32).rearrange("p (a u w) -> p a u w", a=BANK_STRIPS, u=2),
                    in_=pieces[b].bitcast(F32).rearrange("p (a w u) -> p a u w", a=BANK_STRIPS, u=2),
                )
                sorted_words[(key, b)] = pack

        def transpose_chunk(key, pieces, order, codes, scales):
            grouped = stage.tile([P, STRIPS * FEAT], BF16, name="grouped", align_bytes=64)
            filled = []
            for b in range(PIECES):
                bank = banks.tile([P, FEAT], F32, name="bank", tag="bank")
                for j in range(BANK_STRIPS * 2):
                    a, u = divmod(j, 2)
                    if (key, b) in sorted_words:
                        picked = sorted_words[(key, b)][:].bitcast(F32)[:, j * P : (j + 1) * P]
                    else:
                        picked = pieces[b].bitcast(F32)[:, a * 2 * P + u : (a + 1) * 2 * P : 2]
                    nc.tensor.transpose(bank[:, j * P : (j + 1) * P], picked, ident[:])
                filled.append(bank)
            chunks[key] = (grouped, filled, order, codes, scales)

        def empty_banks(key, which):
            grouped, filled, order, codes, scales = chunks[key]
            places = grouped[:].bitcast(F32).rearrange(order, a=BANK_STRIPS, b=PIECES, u=2)
            for b in which:
                nc.scalar.copy(
                    out=places[:, b, :, :, :], in_=filled[b][:].rearrange("p (a u r) -> p a r u", a=BANK_STRIPS, u=2)
                )

        def quantise(key, halves=(0, 1)):
            grouped, filled, order, codes, scales = chunks[key]
            for s in (half * QUANT_STRIPS for half in halves):
                nc.vector.quantize_mx(
                    out=codes[:, s * P : (s + QUANT_STRIPS) * P].bitcast(FP8X4),
                    scales=scales[:, s * P : (s + QUANT_STRIPS) * P],
                    in_=grouped[:, s * FEAT : (s + QUANT_STRIPS) * FEAT],
                )

        def transpose_w(c):
            columns = slice(c * STRIPS * P, (c + 1) * STRIPS * P)
            transpose_chunk(("w", c), w_raw[c], "p (a b r u) -> p b a r u", w_codes[:, columns], w_scales[:, columns])

        def transpose_x(g, c):
            x_codes_tile = operands.tile([P, WINDOW // 4 + STRIPS * P], U32, name="x_codes", align_bytes=64)
            x_scales_tile = operands.tile([P, WINDOW + STRIPS * P], U8, name="x_scales", align_bytes=64)
            x_codes = x_codes_tile[:, 128 // 4 : 128 // 4 + STRIPS * P]
            x_scales = x_scales_tile[:, 192 : 192 + STRIPS * P]
            transpose_chunk((g, c), x_raw[(g, c)], "p (b a r u) -> p b a r u", x_codes, x_scales)
            x_operands[(g, c)] = (x_codes, x_scales)

        def prepare(key):
            empty_banks(key, range(PIECES))
            quantise(key)

        def multiply_tile(g, t, end):
            if (g, t) not in heads_done:
                acc[(g, t)] = sums.tile([P, FEAT], F32, name="acc", tag="acc")
            for head in range(heads_done.get((g, t), 0), end):
                x_codes, x_scales = x_operands[(g, head // X_HEADS)]
                strip = (head % X_HEADS) * TILES + t
                nc.tensor.matmul_mx(
                    out=acc[(g, t)][:],
                    lhsT=x_codes[:, strip * P : (strip + 1) * P].bitcast(FP8X4),
                    lhsT_scale=x_scales[:, strip * P : (strip + 1) * P],
                    rhs=w_codes[:, head * FEAT : (head + 1) * FEAT].bitcast(FP8X4),
                    rhs_scale=w_scales[:, head * FEAT : (head + 1) * FEAT],
                    start=(head == 0),
                    stop=(head == HEADS - 1),
                )
            heads_done[(g, t)] = end

        def multiply(g, end):
            for t in range(TILES):
                multiply_tile(g, t, end)

        def add_bias_to_residual(g, t):
            q_plus_b = rows_pool.tile([P, FEAT], F32, name="q_plus_b")
            nc.gpsimd.tensor_tensor(
                out=q_plus_b[:], in0=q_raw[g][:, t * FEAT : (t + 1) * FEAT], in1=bias_all[:], op=ADD
            )
            residual[(g, t)] = q_plus_b

        def take_sums(g, t):
            x = rows_pool.tile([P, FEAT], F32, name="x")
            row_sum = stats.tile([P, 1], F32, name="row_sum")
            nc.vector.scalar_tensor_tensor(
                out=x[:], in0=acc[(g, t)][:], scalar=0.0, in1=residual[(g, t)][:], op0=ADD, op1=ADD,
                accum_out=row_sum[:],
            )
            minus_mean = stats.tile([P, 1], F32, name="minus_mean")
            nc.gpsimd.tensor_scalar(
                out=minus_mean[:], in0=row_sum[:], scalar1=-1.0 / FEAT, scalar2=0.0, op0=MULT, op1=ADD
            )
            centred[(g, t)] = (x, row_sum, minus_mean)

        def inverse_deviation(g, t):
            x, row_sum, minus_mean = centred[(g, t)]
            squares = rows_pool.tile([P, FEAT], F32, name="squares", bufs=2)
            square_sum = stats.tile([P, 1], F32, name="square_sum")
            nc.scalar.activation(
                out=squares[:], in_=x[:], func=SQUARE, bias=row_sum[:], scale=-1.0 * FEAT, accum_out=square_sum[:]
            )
            inverse = stats.tile([P, 1], F32, name="inverse")
            nc.scalar.activation(
                out=inverse[:], in_=square_sum[:], func=INV_SQRT, bias=eps[:], scale=1.0 / (FEAT * FEAT * FEAT)
            )
            inverses[(g, t)] = inverse

        def scale_by_gamma(g, t):
            x, row_sum, minus_mean = centred[(g, t)]
            scaled = rows_pool.tile([P, FEAT], F32, name="scaled")
            nc.vector.scalar_tensor_tensor(
                out=scaled[:], in0=x[:], scalar=minus_mean[:], in1=gamma_beta[:, 0, :], op0=ADD, op1=MULT
            )
            scaled_rows[(g, t)] = scaled

        def normalise_and_store(g):
            group_rows = out_rows[g * TILES * P : (g + 1) * TILES * P, :].rearrange("(p t) n -> p t n", t=TILES)
            for t in range(TILES):
                scaled, inverse = scaled_rows[(g, t)], inverses[(g, t)]
                parts = 2 if (g == GROUPS - 1 and t == TILES - 1) else 1
                width = FEAT // parts
                for i in range(parts):
                    columns = slice(i * width, (i + 1) * width)
                    nc.vector.scalar_tensor_tensor(
                        out=scaled[:, columns], in0=scaled[:, columns], scalar=inverse[:],
                        in1=gamma_beta[:, 1, columns], op0=MULT, op1=ADD,
                    )
                    nc.sync.dma_start(out=group_rows[:, t, columns], in_=scaled[:, columns])

        transpose_w(0)
        prepare(("w", 0))
        spread_vectors()
        transpose_x(0, 0)
        prepare((0, 0))
        transpose_w(1)
        sort_words(("w", 2), EARLY_SORTS, nc.vector.tensor_copy)
        prepare(("w", 1))
        multiply(0, W_HEADS)
        transpose_w(2)
        sort_words((0, 1), EARLY_SORTS, nc.vector.tensor_copy)
        prepare(("w", 2))
        multiply_tile(0, 0, 2 * W_HEADS)
        transpose_x(0, 1)
        multiply_tile(0, 1, 2 * W_HEADS)
        sort_words(("w", 3), EARLY_SORTS, nc.vector.tensor_copy)
        prepare((0, 1))
        transpose_w(3)
        sort_words((1, 0), VECTOR_SORTS, nc.vector.tensor_copy)
        prepare(("w", 3))
        sort_words((1, 0), SCALAR_SORTS, nc.scalar.copy)
        multiply(0, 3 * W_HEADS)
        for t in range(TILES):
            add_bias_to_residual(0, t)
        for g in range(1, GROUPS):
            before = g - 1
            transpose_x(g, 0)
            sort_words((g, 1), VECTOR_SORTS, nc.vector.tensor_copy)
            empty_banks((g, 0), range(PIECES - 1))
            sort_words((g, 1), SCALAR_SORTS, nc.scalar.copy)
            empty_banks((g, 0), (PIECES - 1,))
            quantise((g, 0), (0,))
            multiply(before, HEADS)
            add_bias_to_residual(g, 0)
            take_sums(before, 0)
            quantise((g, 0), (1,))
            add_bias_to_residual(g, 1)
            take_sums(before, 1)
            scale_by_gamma(before, 0)
            transpose_x(g, 1)
            if g + 1 < GROUPS:
                sort_words((g + 1, 0), VECTOR_SORTS, nc.vector.tensor_copy)
                empty_banks((g, 1), range(PIECES - 1))
                sort_words((g + 1, 0), SCALAR_SORTS, nc.scalar.copy)
                empty_banks((g, 1), (PIECES - 1,))
            else:
                empty_banks((g, 1), range(PIECES))
            quantise((g, 1))
            scale_by_gamma(before, 1)
            for t in range(TILES):
                inverse_deviation(before, t)
            normalise_and_store(before)
            multiply(g, X_HEADS)
        multiply(g, HEADS)
        for t in range(TILES):
            take_sums(g, t)
        for t in range(TILES):
            scale_by_gamma(g, t)
            inverse_deviation(g, t)
        normalise_and_store(g)
